import numpy as np
import ml_dtypes

BF16 = ml_dtypes.bfloat16


def bf(x):
    return np.asarray(x, np.float32).astype(BF16)


def f32(x):
    return np.asarray(x, np.float32)


def f64(x):
    return np.asarray(x).astype(np.float64)


def striped(idx):
    return np.tile(idx.reshape(-1, 16).T, (8, 1))


D, S, K, NN, N = 128, 512, 4, 64, 256
ALPHA, BETA = 0.95, 0.9
P_SPIKE, B_SCALE = 0.1, 0.5


def setup_inputs():
    return {"s_prev": bf(np.random.random((D, S)) < P_SPIKE), "w": bf(np.random.standard_normal((D, K * D)) / np.sqrt(K * D * P_SPIKE)), "b": f32(B_SCALE * np.random.standard_normal((D, 1))), "u": f32(np.random.random((D, NN))), "i_syn": f32(np.random.standard_normal((D, NN))), "offs": striped(np.random.permutation(np.tile(np.arange(S), 2))[:N])}


def reference(s_prev, w, b, u, i_syn, offs):
    idx = offs[:16].T.reshape(-1)
    tab = f64(s_prev)
    wt = f64(w)
    x = np.zeros((D, NN))
    for t in range(K):
        x = x + wt[:, t * D:(t + 1) * D].T @ tab[:, idx[t * NN:(t + 1) * NN]]
    i_new = BETA * f64(i_syn) + (x + f64(b))
    return ALPHA * f64(u) + (1.0 - ALPHA) * i_new

@@ -1,0 +1,55 @@
+import concourse.mybir as mybir
+
+BF16, F32, U16 = mybir.dt.bfloat16, mybir.dt.float32, mybir.dt.uint16
+MULT, ADD = mybir.AluOpType.mult, mybir.AluOpType.add
+
+FEATURES = 128
+NODES = 512
+SLOTS = 4
+UPDATED = 64
+ENTRIES = SLOTS * UPDATED
+SLOT_COLUMNS = UPDATED // 16
+ALPHA, BETA = 0.95, 0.9
+
+FLOPS = 2 * FEATURES * FEATURES * ENTRIES
+
+
+def tile_snnasgnncellmodel_kernel(tc, s_prev, w, b, u, i_syn, offs, out):
+    nc = tc.nc
+    with (
+        tc.tile_pool(name="held", bufs=1) as held,
+        tc.psum_pool(name="psum", bufs=1) as psum,
+    ):
+        offsets = held.tile([FEATURES, ENTRIES // 16], U16, name="offsets")
+        nc.sync.dma_start(offsets[:], offs)
+        spikes = held.tile([FEATURES, NODES], BF16, name="spikes")
+        nc.sync.dma_start(spikes[:], s_prev)
+        weights = held.tile([FEATURES, SLOTS * FEATURES], BF16, name="weights")
+        nc.scalar.dma_start(weights[:], w)
+        bias = held.tile([FEATURES, 1], F32, name="bias")
+        nc.scalar.dma_start(bias[:], b)
+        current = held.tile([FEATURES, UPDATED], F32, name="current")
+        nc.gpsimd.dma_start(current[:], i_syn)
+        potential = held.tile([FEATURES, UPDATED], F32, name="potential")
+        nc.gpsimd.dma_start(potential[:], u)
+
+        decayed = held.tile([FEATURES, UPDATED], F32, name="decayed")
+        nc.vector.tensor_scalar(decayed[:], current[:], BETA, bias[:, 0:1], MULT, ADD)
+        leaked = held.tile([FEATURES, UPDATED], F32, name="leaked")
+        nc.vector.tensor_scalar(leaked[:], potential[:], ALPHA, None, MULT)
+        rest = held.tile([FEATURES, UPDATED], F32, name="rest")
+        nc.vector.scalar_tensor_tensor(rest[:], decayed[:], 1.0 - ALPHA, leaked[:], MULT, ADD)
+
+        projected = psum.tile([FEATURES, UPDATED], F32, name="projected")
+        for t in range(SLOTS):
+            nc.tensor.matmul(
+                projected[:],
+                weights[:, t * FEATURES : (t + 1) * FEATURES],
+                spikes[:].indirect(offsets[:, t * SLOT_COLUMNS : (t + 1) * SLOT_COLUMNS]),
+                start=(t == 0),
+                stop=(t == SLOTS - 1),
+            )
+
+        result = held.tile([FEATURES, UPDATED], F32, name="result")
+        nc.vector.scalar_tensor_tensor(result[:], projected[:], 1.0 - ALPHA, rest[:], MULT, ADD)
+        nc.sync.dma_start(out, result[:])

@@ -29,9 +29,9 @@ def tile_snnasgnncellmodel_kernel(tc, s_prev, w, b, u, i_syn, offs, out):
         bias = held.tile([FEATURES, 1], F32, name="bias")
         nc.scalar.dma_start(bias[:], b)
         current = held.tile([FEATURES, UPDATED], F32, name="current")
-        nc.gpsimd.dma_start(current[:], i_syn)
+        nc.sync.dma_start(current[:], i_syn)
         potential = held.tile([FEATURES, UPDATED], F32, name="potential")
-        nc.gpsimd.dma_start(potential[:], u)
+        nc.scalar.dma_start(potential[:], u)
 
         decayed = held.tile([FEATURES, UPDATED], F32, name="decayed")
         nc.vector.tensor_scalar(decayed[:], current[:], BETA, bias[:, 0:1], MULT, ADD)

@@ -10,6 +10,8 @@ UPDATED = 64
 ENTRIES = SLOTS * UPDATED
 SLOT_COLUMNS = UPDATED // 16
 ALPHA, BETA = 0.95, 0.9
+BANK = 512
+WARMING_MATMULS = 2 * 1024 // BANK
 
 FLOPS = 2 * FEATURES * FEATURES * ENTRIES
 
@@ -32,6 +34,12 @@ def tile_snnasgnncellmodel_kernel(tc, s_prev, w, b, u, i_syn, offs, out):
         nc.sync.dma_start(current[:], i_syn)
         potential = held.tile([FEATURES, UPDATED], F32, name="potential")
         nc.scalar.dma_start(potential[:], u)
+
+        zeros = held.tile([FEATURES, BANK], BF16, name="zeros")
+        nc.vector.memset(zeros[:], 0.0)
+        unused = psum.tile([FEATURES, BANK], F32, name="unused")
+        for i in range(WARMING_MATMULS):
+            nc.tensor.matmul(unused[:], zeros[:, 0:FEATURES], zeros[:], start=True, stop=True)
 
         decayed = held.tile([FEATURES, UPDATED], F32, name="decayed")
         nc.vector.tensor_scalar(decayed[:], current[:], BETA, bias[:, 0:1], MULT, ADD)

@@ -10,8 +10,6 @@ UPDATED = 64
 ENTRIES = SLOTS * UPDATED
 SLOT_COLUMNS = UPDATED // 16
 ALPHA, BETA = 0.95, 0.9
-BANK = 512
-WARMING_MATMULS = 2 * 1024 // BANK
 
 FLOPS = 2 * FEATURES * FEATURES * ENTRIES
 
@@ -28,33 +26,29 @@ def tile_snnasgnncellmodel_kernel(tc, s_prev, w, b, u, i_syn, offs, out):
         nc.sync.dma_start(spikes[:], s_prev)
         weights = held.tile([FEATURES, SLOTS * FEATURES], BF16, name="weights")
         nc.scalar.dma_start(weights[:], w)
-        bias = held.tile([FEATURES, 1], F32, name="bias")
-        nc.scalar.dma_start(bias[:], b)
+        bias_row = held.tile([1, FEATURES], F32, name="bias_row")
+        nc.scalar.dma_start(bias_row[:], b.rearrange("m one -> one m"))
         current = held.tile([FEATURES, UPDATED], F32, name="current")
         nc.sync.dma_start(current[:], i_syn)
         potential = held.tile([FEATURES, UPDATED], F32, name="potential")
         nc.scalar.dma_start(potential[:], u)
 
-        zeros = held.tile([FEATURES, BANK], BF16, name="zeros")
-        nc.vector.memset(zeros[:], 0.0)
-        unused = psum.tile([FEATURES, BANK], F32, name="unused")
-        for i in range(WARMING_MATMULS):
-            nc.tensor.matmul(unused[:], zeros[:, 0:FEATURES], zeros[:], start=True, stop=True)
+        ones_row = held.tile([1, UPDATED], F32, name="ones_row")
+        nc.vector.memset(ones_row[:], 1.0)
 
-        decayed = held.tile([FEATURES, UPDATED], F32, name="decayed")
-        nc.vector.tensor_scalar(decayed[:], current[:], BETA, bias[:, 0:1], MULT, ADD)
         leaked = held.tile([FEATURES, UPDATED], F32, name="leaked")
         nc.vector.tensor_scalar(leaked[:], potential[:], ALPHA, None, MULT)
         rest = held.tile([FEATURES, UPDATED], F32, name="rest")
-        nc.vector.scalar_tensor_tensor(rest[:], decayed[:], 1.0 - ALPHA, leaked[:], MULT, ADD)
+        nc.vector.scalar_tensor_tensor(rest[:], current[:], (1.0 - ALPHA) * BETA, leaked[:], MULT, ADD)
 
         projected = psum.tile([FEATURES, UPDATED], F32, name="projected")
+        nc.tensor.matmul(projected[:], bias_row[:], ones_row[:], start=True, stop=False)
         for t in range(SLOTS):
             nc.tensor.matmul(
                 projected[:],
                 weights[:, t * FEATURES : (t + 1) * FEATURES],
                 spikes[:].indirect(offsets[:, t * SLOT_COLUMNS : (t + 1) * SLOT_COLUMNS]),
-                start=(t == 0),
+                start=False,
                 stop=(t == SLOTS - 1),
             )
 

@@ -26,29 +26,27 @@ def tile_snnasgnncellmodel_kernel(tc, s_prev, w, b, u, i_syn, offs, out):
         nc.sync.dma_start(spikes[:], s_prev)
         weights = held.tile([FEATURES, SLOTS * FEATURES], BF16, name="weights")
         nc.scalar.dma_start(weights[:], w)
-        bias_row = held.tile([1, FEATURES], F32, name="bias_row")
-        nc.scalar.dma_start(bias_row[:], b.rearrange("m one -> one m"))
+        bias = held.tile([FEATURES, 1], F32, name="bias")
+        nc.scalar.dma_start(bias[:], b)
         current = held.tile([FEATURES, UPDATED], F32, name="current")
         nc.sync.dma_start(current[:], i_syn)
         potential = held.tile([FEATURES, UPDATED], F32, name="potential")
         nc.scalar.dma_start(potential[:], u)
 
-        ones_row = held.tile([1, UPDATED], F32, name="ones_row")
-        nc.vector.memset(ones_row[:], 1.0)
-
-        leaked = held.tile([FEATURES, UPDATED], F32, name="leaked")
-        nc.vector.tensor_scalar(leaked[:], potential[:], ALPHA, None, MULT)
+        decayed = held.tile([FEATURES, UPDATED], F32, name="decayed")
+        nc.vector.tensor_scalar(decayed[:], current[:], BETA, bias[:, 0:1], MULT, ADD)
+        share = held.tile([FEATURES, UPDATED], F32, name="share")
+        nc.vector.tensor_scalar(share[:], decayed[:], 1.0 - ALPHA, None, MULT)
         rest = held.tile([FEATURES, UPDATED], F32, name="rest")
-        nc.vector.scalar_tensor_tensor(rest[:], current[:], (1.0 - ALPHA) * BETA, leaked[:], MULT, ADD)
+        nc.vector.scalar_tensor_tensor(rest[:], potential[:], ALPHA, share[:], MULT, ADD)
 
         projected = psum.tile([FEATURES, UPDATED], F32, name="projected")
-        nc.tensor.matmul(projected[:], bias_row[:], ones_row[:], start=True, stop=False)
         for t in range(SLOTS):
             nc.tensor.matmul(
                 projected[:],
                 weights[:, t * FEATURES : (t + 1) * FEATURES],
                 spikes[:].indirect(offsets[:, t * SLOT_COLUMNS : (t + 1) * SLOT_COLUMNS]),
-                start=False,
+                start=(t == 0),
                 stop=(t == SLOTS - 1),
             )
 

@@ -24,29 +24,31 @@ def tile_snnasgnncellmodel_kernel(tc, s_prev, w, b, u, i_syn, offs, out):
         nc.sync.dma_start(offsets[:], offs)
         spikes = held.tile([FEATURES, NODES], BF16, name="spikes")
         nc.sync.dma_start(spikes[:], s_prev)
+        bias_row = held.tile([1, FEATURES], F32, name="bias_row")
+        nc.scalar.dma_start(bias_row[:], b.rearrange("m one -> one m"))
         weights = held.tile([FEATURES, SLOTS * FEATURES], BF16, name="weights")
         nc.scalar.dma_start(weights[:], w)
-        bias = held.tile([FEATURES, 1], F32, name="bias")
-        nc.scalar.dma_start(bias[:], b)
         current = held.tile([FEATURES, UPDATED], F32, name="current")
         nc.sync.dma_start(current[:], i_syn)
         potential = held.tile([FEATURES, UPDATED], F32, name="potential")
         nc.scalar.dma_start(potential[:], u)
 
-        decayed = held.tile([FEATURES, UPDATED], F32, name="decayed")
-        nc.vector.tensor_scalar(decayed[:], current[:], BETA, bias[:, 0:1], MULT, ADD)
+        ones_row = held.tile([1, UPDATED], F32, name="ones_row")
+        nc.vector.memset(ones_row[:], 1.0)
+
         share = held.tile([FEATURES, UPDATED], F32, name="share")
-        nc.vector.tensor_scalar(share[:], decayed[:], 1.0 - ALPHA, None, MULT)
+        nc.vector.tensor_scalar(share[:], current[:], (1.0 - ALPHA) * BETA, None, MULT)
         rest = held.tile([FEATURES, UPDATED], F32, name="rest")
         nc.vector.scalar_tensor_tensor(rest[:], potential[:], ALPHA, share[:], MULT, ADD)
 
         projected = psum.tile([FEATURES, UPDATED], F32, name="projected")
+        nc.tensor.matmul(projected[:], bias_row[:], ones_row[:], start=True, stop=False)
         for t in range(SLOTS):
             nc.tensor.matmul(
                 projected[:],
                 weights[:, t * FEATURES : (t + 1) * FEATURES],
                 spikes[:].indirect(offsets[:, t * SLOT_COLUMNS : (t + 1) * SLOT_COLUMNS]),
-                start=(t == 0),
+                start=False,
                 stop=(t == SLOTS - 1),
             )
 

@@ -20,12 +20,12 @@ def tile_snnasgnncellmodel_kernel(tc, s_prev, w, b, u, i_syn, offs, out):
         tc.tile_pool(name="held", bufs=1) as held,
         tc.psum_pool(name="psum", bufs=1) as psum,
     ):
+        bias_row = held.tile([1, FEATURES], F32, name="bias_row")
+        nc.sync.dma_start(bias_row[:], b.rearrange("m one -> one m"))
         offsets = held.tile([FEATURES, ENTRIES // 16], U16, name="offsets")
         nc.sync.dma_start(offsets[:], offs)
         spikes = held.tile([FEATURES, NODES], BF16, name="spikes")
         nc.sync.dma_start(spikes[:], s_prev)
-        bias_row = held.tile([1, FEATURES], F32, name="bias_row")
-        nc.scalar.dma_start(bias_row[:], b.rearrange("m one -> one m"))
         weights = held.tile([FEATURES, SLOTS * FEATURES], BF16, name="weights")
         nc.scalar.dma_start(weights[:], w)
         current = held.tile([FEATURES, UPDATED], F32, name="current")

@@ -29,9 +29,9 @@ def tile_snnasgnncellmodel_kernel(tc, s_prev, w, b, u, i_syn, offs, out):
         weights = held.tile([FEATURES, SLOTS * FEATURES], BF16, name="weights")
         nc.scalar.dma_start(weights[:], w)
         current = held.tile([FEATURES, UPDATED], F32, name="current")
-        nc.sync.dma_start(current[:], i_syn)
+        nc.scalar.dma_start(current[:], i_syn)
         potential = held.tile([FEATURES, UPDATED], F32, name="potential")
-        nc.scalar.dma_start(potential[:], u)
+        nc.sync.dma_start(potential[:], u)
 
         ones_row = held.tile([1, UPDATED], F32, name="ones_row")
         nc.vector.memset(ones_row[:], 1.0)

@@ -24,13 +24,15 @@ def tile_snnasgnncellmodel_kernel(tc, s_prev, w, b, u, i_syn, offs, out):
         nc.sync.dma_start(bias_row[:], b.rearrange("m one -> one m"))
         offsets = held.tile([FEATURES, ENTRIES // 16], U16, name="offsets")
         nc.sync.dma_start(offsets[:], offs)
-        spikes = held.tile([FEATURES, NODES], BF16, name="spikes")
+        spikes = held.tile([FEATURES, NODES], BF16, name="spikes", align_bytes=2 * NODES)
         nc.sync.dma_start(spikes[:], s_prev)
-        weights = held.tile([FEATURES, SLOTS * FEATURES], BF16, name="weights")
+        weights = held.tile(
+            [FEATURES, SLOTS * FEATURES], BF16, name="weights", align_bytes=2 * SLOTS * FEATURES
+        )
         nc.scalar.dma_start(weights[:], w)
-        current = held.tile([FEATURES, UPDATED], F32, name="current")
+        current = held.tile([FEATURES, UPDATED], F32, name="current", align_bytes=4 * UPDATED)
         nc.scalar.dma_start(current[:], i_syn)
-        potential = held.tile([FEATURES, UPDATED], F32, name="potential")
+        potential = held.tile([FEATURES, UPDATED], F32, name="potential", align_bytes=4 * UPDATED)
         nc.sync.dma_start(potential[:], u)
 
         ones_row = held.tile([1, UPDATED], F32, name="ones_row")
@@ -52,6 +54,6 @@ def tile_snnasgnncellmodel_kernel(tc, s_prev, w, b, u, i_syn, offs, out):
                 stop=(t == SLOTS - 1),
             )
 
-        result = held.tile([FEATURES, UPDATED], F32, name="result")
+        result = held.tile([FEATURES, UPDATED], F32, name="result", align_bytes=4 * UPDATED)
         nc.vector.scalar_tensor_tensor(result[:], projected[:], 1.0 - ALPHA, rest[:], MULT, ADD)
         nc.sync.dma_start(out, result[:])

@@ -21,36 +21,38 @@ def tile_snnasgnncellmodel_kernel(tc, s_prev, w, b, u, i_syn, offs, out):
         tc.psum_pool(name="psum", bufs=1) as psum,
     ):
         bias_row = held.tile([1, FEATURES], F32, name="bias_row")
-        nc.sync.dma_start(bias_row[:], b.rearrange("m one -> one m"))
         offsets = held.tile([FEATURES, ENTRIES // 16], U16, name="offsets")
-        nc.sync.dma_start(offsets[:], offs)
         spikes = held.tile([FEATURES, NODES], BF16, name="spikes", align_bytes=2 * NODES)
-        nc.sync.dma_start(spikes[:], s_prev)
         weights = held.tile(
             [FEATURES, SLOTS * FEATURES], BF16, name="weights", align_bytes=2 * SLOTS * FEATURES
         )
-        nc.scalar.dma_start(weights[:], w)
         current = held.tile([FEATURES, UPDATED], F32, name="current", align_bytes=4 * UPDATED)
-        nc.scalar.dma_start(current[:], i_syn)
         potential = held.tile([FEATURES, UPDATED], F32, name="potential", align_bytes=4 * UPDATED)
+
+        nc.sync.dma_start(bias_row[:], b.rearrange("m one -> one m"))
+        nc.sync.dma_start(offsets[:], offs)
+        nc.sync.dma_start(spikes[:], s_prev)
+        nc.scalar.dma_start(weights[:], w)
+        nc.scalar.dma_start(current[:], i_syn)
         nc.sync.dma_start(potential[:], u)
 
-        ones_row = held.tile([1, UPDATED], F32, name="ones_row")
-        nc.vector.memset(ones_row[:], 1.0)
+        one_number = held.tile([1, 1], F32, name="one_number")
+        nc.vector.memset(one_number[:], 1.0 - ALPHA)
+        bias = psum.tile([FEATURES, 1], F32, name="bias")
+        nc.tensor.matmul(bias[:], bias_row[:], one_number[:])
 
         share = held.tile([FEATURES, UPDATED], F32, name="share")
-        nc.vector.tensor_scalar(share[:], current[:], (1.0 - ALPHA) * BETA, None, MULT)
+        nc.vector.tensor_scalar(share[:], current[:], (1.0 - ALPHA) * BETA, bias[:], MULT, ADD)
         rest = held.tile([FEATURES, UPDATED], F32, name="rest")
         nc.vector.scalar_tensor_tensor(rest[:], potential[:], ALPHA, share[:], MULT, ADD)
 
         projected = psum.tile([FEATURES, UPDATED], F32, name="projected")
-        nc.tensor.matmul(projected[:], bias_row[:], ones_row[:], start=True, stop=False)
         for t in range(SLOTS):
             nc.tensor.matmul(
                 projected[:],
                 weights[:, t * FEATURES : (t + 1) * FEATURES],
                 spikes[:].indirect(offsets[:, t * SLOT_COLUMNS : (t + 1) * SLOT_COLUMNS]),
-                start=False,
+                start=(t == 0),
                 stop=(t == SLOTS - 1),
             )
 

@@ -30,10 +30,10 @@ def tile_snnasgnncellmodel_kernel(tc, s_prev, w, b, u, i_syn, offs, out):
         potential = held.tile([FEATURES, UPDATED], F32, name="potential", align_bytes=4 * UPDATED)
 
         nc.sync.dma_start(bias_row[:], b.rearrange("m one -> one m"))
+        nc.scalar.dma_start(spikes[:], s_prev)
         nc.sync.dma_start(offsets[:], offs)
-        nc.sync.dma_start(spikes[:], s_prev)
         nc.scalar.dma_start(weights[:], w)
-        nc.scalar.dma_start(current[:], i_syn)
+        nc.sync.dma_start(current[:], i_syn)
         nc.sync.dma_start(potential[:], u)
 
         one_number = held.tile([1, 1], F32, name="one_number")
@@ -41,9 +41,9 @@ def tile_snnasgnncellmodel_kernel(tc, s_prev, w, b, u, i_syn, offs, out):
         bias = psum.tile([FEATURES, 1], F32, name="bias")
         nc.tensor.matmul(bias[:], bias_row[:], one_number[:])
 
-        share = held.tile([FEATURES, UPDATED], F32, name="share")
+        share = held.tile([FEATURES, UPDATED], F32, name="share", align_bytes=4 * UPDATED)
         nc.vector.tensor_scalar(share[:], current[:], (1.0 - ALPHA) * BETA, bias[:], MULT, ADD)
-        rest = held.tile([FEATURES, UPDATED], F32, name="rest")
+        rest = held.tile([FEATURES, UPDATED], F32, name="rest", align_bytes=4 * UPDATED)
         nc.vector.scalar_tensor_tensor(rest[:], potential[:], ALPHA, share[:], MULT, ADD)
 
         projected = psum.tile([FEATURES, UPDATED], F32, name="projected")

import concourse.mybir as mybir

BF16, F32, U16 = mybir.dt.bfloat16, mybir.dt.float32, mybir.dt.uint16
MULT, ADD = mybir.AluOpType.mult, mybir.AluOpType.add

FEATURES = 128
NODES = 512
SLOTS = 4
UPDATED = 64
ENTRIES = SLOTS * UPDATED
SLOT_COLUMNS = UPDATED // 16
ALPHA, BETA = 0.95, 0.9

FLOPS = 2 * FEATURES * FEATURES * ENTRIES


def tile_snnasgnncellmodel_kernel(tc, s_prev, w, b, u, i_syn, offs, out):
    nc = tc.nc
    with (
        tc.tile_pool(name="held", bufs=1) as held,
        tc.psum_pool(name="psum", bufs=1) as psum,
    ):
        bias_row = held.tile([1, FEATURES], F32, name="bias_row")
        offsets = held.tile([FEATURES, ENTRIES // 16], U16, name="offsets")
        spikes = held.tile([FEATURES, NODES], BF16, name="spikes", align_bytes=2 * NODES)
        weights = held.tile(
            [FEATURES, SLOTS * FEATURES], BF16, name="weights", align_bytes=2 * SLOTS * FEATURES
        )
        current = held.tile([FEATURES, UPDATED], F32, name="current", align_bytes=4 * UPDATED)
        potential = held.tile([FEATURES, UPDATED], F32, name="potential", align_bytes=4 * UPDATED)

        nc.sync.dma_start(bias_row[:], b.rearrange("m one -> one m"))
        nc.scalar.dma_start(spikes[:], s_prev)
        nc.sync.dma_start(offsets[:], offs)
        nc.scalar.dma_start(weights[:], w)
        nc.sync.dma_start(current[:], i_syn)
        nc.sync.dma_start(potential[:], u)

        one_number = held.tile([1, 1], F32, name="one_number")
        nc.vector.memset(one_number[:], 1.0 - ALPHA)
        bias = psum.tile([FEATURES, 1], F32, name="bias")
        nc.tensor.matmul(bias[:], bias_row[:], one_number[:])

        share = held.tile([FEATURES, UPDATED], F32, name="share", align_bytes=4 * UPDATED)
        nc.vector.tensor_scalar(share[:], current[:], (1.0 - ALPHA) * BETA, bias[:], MULT, ADD)
        rest = held.tile([FEATURES, UPDATED], F32, name="rest", align_bytes=4 * UPDATED)
        nc.vector.scalar_tensor_tensor(rest[:], potential[:], ALPHA, share[:], MULT, ADD)

        projected = psum.tile([FEATURES, UPDATED], F32, name="projected")
        for t in range(SLOTS):
            nc.tensor.matmul(
                projected[:],
                weights[:, t * FEATURES : (t + 1) * FEATURES],
                spikes[:].indirect(offsets[:, t * SLOT_COLUMNS : (t + 1) * SLOT_COLUMNS]),
                start=(t == 0),
                stop=(t == SLOTS - 1),
            )

        result = held.tile([FEATURES, UPDATED], F32, name="result", align_bytes=4 * UPDATED)
        nc.vector.scalar_tensor_tensor(result[:], projected[:], 1.0 - ALPHA, rest[:], MULT, ADD)
        nc.sync.dma_start(out, result[:])
